import numpy as np
import ml_dtypes


def mxq(x, axis, fmt="e4m3"):
    dtype, down = {"e4m3": (ml_dtypes.float8_e4m3fn, 7), "e5m2": (ml_dtypes.float8_e5m2, 14)}[fmt]
    v = np.moveaxis(np.asarray(x, np.float32).astype(ml_dtypes.bfloat16).astype(np.float64), axis, -1)
    blocks = v.reshape(v.shape[:-1] + (-1, 32))
    amax = np.abs(blocks).max(-1, keepdims=True)
    byte = np.maximum(np.where(amax > 0, np.frexp(amax)[1] - 1 + 127, 0) - down, 1)
    scale = np.exp2(byte - 127.0)
    codes = (blocks / scale).astype(np.float32).astype(dtype).astype(np.float64)
    return np.moveaxis((codes * scale).reshape(v.shape), -1, axis)


WIDE = False


def mx_kscale(k):
    if not WIDE:
        return np.ones(k)
    levels = np.array([10, -10, 5, -5, 0])
    if k % 512:
        return np.exp2(np.random.permutation(np.resize(levels, k // 32))).repeat(32)
    a = np.empty((k // 512, 16))
    for p in range(k // 512):
        a[p, :8] = np.random.permutation(np.resize(levels, 8))
        for g in range(8):
            far = levels[np.abs(levels - a[p, g]) >= 10]
            a[p, g + 8] = far[np.random.randint(len(far))]
    return np.exp2(a.ravel()).repeat(32)


BF16 = ml_dtypes.bfloat16


def bf(x):
    return np.asarray(x, np.float32).astype(BF16)


def f64(x):
    return np.asarray(x).astype(np.float64)


B, S, E, P, H = 4, 2048, 1024, 128, 4
D = P // H


def rope(x):
    inv_freq = 1.0 / (10000.0 ** (f64(np.arange(0, D, 2)) / D))
    t = f64(np.arange(S))
    freqs = np.repeat(t[:, None] * inv_freq[None, :], 2, axis=-1)
    cos, sin = np.cos(freqs), np.sin(freqs)
    xp = x.reshape(*x.shape[:-1], D // 2, 2)
    rot = np.stack((-xp[..., 1], xp[..., 0]), axis=-1).reshape(x.shape)
    return x * cos + rot * sin


def setup_inputs():
    s = mx_kscale(E)
    return {"emb": bf(np.random.standard_normal((B, S, E)) * s),
            "W1": bf(np.random.standard_normal((P, E)) * 0.6 / np.sqrt(E) / s),
            "W2": bf(np.random.standard_normal((P, E)) * 0.6 / np.sqrt(E) / s),
            "W3": bf(np.random.standard_normal((P, E)) * 2.0 / np.sqrt(E) / s)}


def reference(emb, W1, W2, W3):
    xq = mxq(f64(emb), 2, "e4m3")
    q = (xq @ mxq(f64(W1), 1, "e4m3").T).reshape(B, H, S, D)
    k = (xq @ mxq(f64(W2), 1, "e4m3").T).reshape(B, H, S, D)
    v = (xq @ mxq(f64(W3), 1, "e4m3").T).reshape(B, H, S, D)
    return rope(q), rope(k), v

@@ -1,0 +1,283 @@
+from contextlib import ExitStack
+
+import concourse.mybir as mybir
+from concourse.masks import make_identity
+
+F32 = mybir.dt.float32
+BF16 = mybir.dt.bfloat16
+I32 = mybir.dt.int32
+U32 = mybir.dt.uint32
+U8 = mybir.dt.uint8
+FP8X4 = mybir.dt.float8_e4m3fn_x4
+ALU = mybir.AluOpType
+ACT = mybir.ActivationFunctionType
+
+P = 128
+E = 1024
+TOKENS = 8192
+FLOPS = 2 * TOKENS * E * 384
+PI = 3.141592653589793
+NFREQ = 16
+CHUNKS = 16
+BATCHES = 32
+AHEAD = 10
+
+
+def round_bits(x, bits):
+    k = 1.0
+    while x * k < 2.0 ** (bits - 1):
+        k = k * 2.0
+    return round(x * k) / k
+
+
+PHI = [10000.0 ** (-i / 16.0) / (2.0 * PI) for i in range(NFREQ)]
+PHI_HI = [round_bits(v, 12) for v in PHI]
+PHI_LO = [PHI[i] - PHI_HI[i] for i in range(NFREQ)]
+
+
+def tile_attention_pa_t_kernel(tc, emb, W1, W2, W3, out_0, out_1, out_2):
+    nc = tc.nc
+    emb_v = emb.rearrange("b (h p j) k -> (b h) p (j k)", h=4, p=P, j=4)
+    out_v = [o.rearrange("b h (a x) d -> (b h) a (x d)", x=16) for o in (out_0, out_1, out_2)]
+
+    with ExitStack() as ctx:
+        const = ctx.enter_context(tc.tile_pool(name="const", bufs=1))
+        xpool = ctx.enter_context(tc.tile_pool(name="xpool", bufs=AHEAD))
+        gpool = ctx.enter_context(tc.tile_pool(name="gpool", bufs=4))
+        kpool = ctx.enter_context(tc.tile_pool(name="kpool", bufs=5))
+        mpool = ctx.enter_context(tc.tile_pool(name="mpool", bufs=4))
+        ypool = ctx.enter_context(tc.tile_pool(name="ypool", bufs=6))
+        ps_t = ctx.enter_context(tc.psum_pool(name="ps_t", bufs=4))
+        ps_qk = ctx.enter_context(tc.psum_pool(name="ps_qk", bufs=2))
+        ps_v = ctx.enter_context(tc.psum_pool(name="ps_v", bufs=2))
+
+        s_i = const.tile([P, 16], I32)
+        nc.gpsimd.iota(s_i[:], pattern=[[1, 16]], base=0, channel_multiplier=16)
+        ident = const.tile([P, P], F32)
+        make_identity(nc, ident[:])
+        ctx.enter_context(tc.manual_schedule())
+
+        state = {}
+
+        def load(n):
+            x = xpool.tile([P, 4, E], BF16, tag="x")
+            state[("x", n)] = x
+            if n > 0:
+                nc.sync.dma_start(out=x[:].rearrange("p j k -> p (j k)"), in_=emb_v[n])
+
+        def load_half(bb):
+            x = state[("x", 0)]
+            nc.sync.dma_start(
+                out=x[:, 2 * bb:2 * bb + 2, :].rearrange("p j k -> p (j k)"),
+                in_=emb_v[0][:, 2 * bb * E:(2 * bb + 2) * E],
+            )
+
+        w_raw = const.tile([P, 3, E], BF16)
+        w_aps = (W1, W2, W3)
+        load(0)
+        nc.sync.dma_start(out=w_raw[:, 0, :], in_=w_aps[0])
+        nc.sync.dma_start(out=w_raw[:, 1, :], in_=w_aps[1])
+        load_half(0)
+        nc.sync.dma_start(out=w_raw[:, 2, :], in_=w_aps[2])
+        load_half(1)
+        for n in range(1, AHEAD):
+            load(n)
+
+        zero = const.tile([P, 1], F32)
+        nc.vector.memset(zero[:], 0.0)
+        warm = const.tile([P, 1], F32)
+        nc.scalar.activation(out=warm[:], in_=zero[:], func=ACT.Sin, scale=1.0)
+        s_f = const.tile([P, 16], F32)
+        nc.vector.tensor_copy(out=s_f[:], in_=s_i[:])
+        th = const.tile([P, 16, NFREQ], F32)
+        tl = const.tile([P, 16, NFREQ], F32)
+        for i in range(NFREQ):
+            nc.vector.tensor_scalar_mul(out=th[:, :, i], in0=s_f[:], scalar1=PHI_HI[i])
+            nc.scalar.mul(out=tl[:, :, i], in_=s_f[:], mul=PHI_LO[i])
+        tq = const.tile([P, 256], F32)
+        th2 = th[:].rearrange("p m i -> p (m i)")
+        tl2 = tl[:].rearrange("p m i -> p (m i)")
+        nc.vector.scalar_tensor_tensor(out=tq[:], in0=th2, scalar=0.25, in1=tl2, op0=ALU.add, op1=ALU.add)
+        n_i = const.tile([P, 256], I32)
+        nc.vector.tensor_copy(out=n_i[:], in_=tq[:])
+        fr = const.tile([P, 256], F32)
+        nc.vector.tensor_tensor(out=fr[:], in0=th2, in1=n_i[:], op=ALU.subtract)
+        fr2 = const.tile([P, 256], F32)
+        nc.vector.tensor_tensor(out=fr2[:], in0=fr[:], in1=tl2, op=ALU.add)
+        hs = const.tile([P, 256], F32)
+        qs = const.tile([P, 256], F32)
+        hs2 = const.tile([P, 256], F32)
+        qs2 = const.tile([P, 256], F32)
+
+        def tables_scalar():
+            nc.scalar.activation(out=hs[:], in_=fr2[:], func=ACT.Sin, scale=PI)
+            nc.scalar.activation(out=qs[:], in_=fr2[:], func=ACT.Sin, scale=PI / 2.0)
+            nc.scalar.square(out=hs2[:], in_=hs[:])
+            nc.scalar.square(out=qs2[:], in_=qs[:])
+
+        ctab = const.tile([P, 4, P], F32)
+        stab = const.tile([P, 4, P], F32)
+
+        def tables_vector():
+            cpf = const.tile([P, 256], F32)
+            nc.vector.tensor_scalar(out=cpf[:], in0=qs2[:], scalar1=-4.0, scalar2=2.0, op0=ALU.mult, op1=ALU.add)
+            ctab_v = ctab[:].rearrange("p j (n two) -> p (j n) two", two=2)
+            stab_v = stab[:].rearrange("p j (n two) -> p (j n) two", two=2)
+            nc.vector.tensor_scalar(
+                out=ctab_v, in0=hs2[:].unsqueeze(2).to_broadcast([P, 256, 2]),
+                scalar1=-2.0, scalar2=1.0, op0=ALU.mult, op1=ALU.add,
+            )
+            nc.vector.tensor_tensor(out=stab_v[:, :, 1], in0=hs[:], in1=cpf[:], op=ALU.mult)
+            nc.vector.tensor_scalar_mul(out=stab_v[:, :, 0], in0=stab_v[:, :, 1], scalar1=-1.0)
+
+        w_grp = const.tile([P, 2, 384, 4], BF16, align_bytes=64)
+        w_grp32 = w_grp[:].bitcast(F32)
+        w_raw32 = w_raw[:].bitcast(F32)
+        w_codes = const.tile([P, 2, 384], U32, align_bytes=64)
+        w_scales = const.tile([P, 2, 384], U8, align_bytes=64)
+
+        def w_transpose(w):
+            tp = ps_t.tile([P, 4, P], F32, tag="tp")
+            for wb in range(4):
+                nc.tensor.transpose(out=tp[:, wb, :], in_=w_raw32[:, w, 256 * (wb // 2) + wb % 2:256 * (wb // 2 + 1):2], identity=ident[:])
+            state[("wtp", w)] = tp
+
+        def w_copy(w):
+            nc.vector.tensor_copy(
+                out=w_grp32[:, :, w * P:(w + 1) * P, :],
+                in_=state[("wtp", w)][:].rearrange("p (g u) r -> p g r u", u=2),
+            )
+
+        def w_quantise(lo, hi):
+            for g in range(2):
+                nc.vector.quantize_mx(
+                    out=w_codes[:, g, lo:hi].bitcast(FP8X4),
+                    scales=w_scales[:, g, lo:hi],
+                    in_=w_grp[:, g, lo:hi, :].rearrange("p f t -> p (f t)"),
+                )
+
+        def transposes(b):
+            n, bb = divmod(b, 2)
+            x32 = state[("x", n)][:].bitcast(F32)
+            grp = gpool.tile([P, 2, 2, P, 4], BF16, tag="grp", align_bytes=64)
+            grp32 = grp[:].bitcast(F32)
+            for jj in range(2):
+                tp = ps_t.tile([P, 4, P], F32, tag="tp")
+                for wb in range(4):
+                    nc.tensor.transpose(
+                        out=tp[:, wb, :], in_=x32[:, 2 * bb + jj, 256 * (wb // 2) + wb % 2:256 * (wb // 2 + 1):2], identity=ident[:]
+                    )
+                nc.scalar.copy(out=grp32[:, jj], in_=tp[:].rearrange("p (g u) r -> p g r u", u=2))
+            state[("grp", b)] = grp
+
+        def quantise(b):
+            grp = state[("grp", b)]
+            codes = kpool.tile([P, 512], U32, tag="codes", align_bytes=64)
+            scales = kpool.tile([P, 512], U8, tag="scales", align_bytes=64)
+            nc.vector.quantize_mx(
+                out=codes[:].bitcast(FP8X4), scales=scales[:],
+                in_=grp[:].rearrange("p a g r t -> p (a g r t)"),
+            )
+            state[("q", b)] = (codes, scales)
+
+        def products(b):
+            n, bb = divmod(b, 2)
+            codes, scales = state[("q", b)]
+            qk = ps_qk.tile([P, 2, 256], F32, tag="qk")
+            vb = ps_v.tile([P, 2, P], F32, tag="vb")
+            for jj in range(2):
+                for g in range(2):
+                    c0 = (jj * 2 + g) * P
+                    for dst, lo, hi in ((qk[:, jj, :], 0, 256), (vb[:, jj, :], 256, 384)):
+                        nc.tensor.matmul_mx(
+                            out=dst,
+                            lhsT=codes[:, c0:c0 + P].bitcast(FP8X4),
+                            lhsT_scale=scales[:, c0:c0 + P],
+                            rhs=w_codes[:, g, lo:hi].bitcast(FP8X4),
+                            rhs_scale=w_scales[:, g, lo:hi],
+                            start=(g == 0), stop=(g == 1),
+                        )
+            state[("qk", b)] = qk
+            if bb == 0:
+                yv = ypool.tile([P, 4, P], F32, tag="yv")
+                state[("yv", n)] = yv
+            nc.scalar.copy(out=state[("yv", n)][:, 2 * bb:2 * bb + 2, :], in_=vb[:])
+            if bb == 1:
+                nc.sync.dma_start(out=out_v[2][n], in_=state[("yv", n)][:].rearrange("p j f -> p (j f)"))
+
+        def rotate(b):
+            n, bb = divmod(b, 2)
+            qk = state[("qk", b)]
+            shape5 = [P, 2, 2, 64, 2]
+            m1 = mpool.tile([P, 512], F32, tag="m1")
+            m2 = mpool.tile([P, 512], F32, tag="m2")
+            js = slice(2 * bb, 2 * bb + 2)
+            ct = ctab[:, js, :].rearrange("p a (n two) -> p a n two", two=2).unsqueeze(2).to_broadcast(shape5)
+            st = stab[:, js, :].rearrange("p a (n two) -> p a n two", two=2).unsqueeze(2).to_broadcast(shape5)
+            x5 = qk[:].rearrange("p a (q n two) -> p a q n two", q=2, two=2)
+            nc.vector.tensor_tensor(
+                out=m1[:].rearrange("p (a q n two) -> p a q n two", a=2, q=2, two=2), in0=x5, in1=ct, op=ALU.mult
+            )
+            nc.vector.tensor_tensor(
+                out=m2[:].rearrange("p (a q n two) -> p a q n two", a=2, q=2, two=2),
+                in0=x5[:, :, :, :, ::-1], in1=st, op=ALU.mult,
+            )
+            state[("m", b)] = (m1, m2)
+
+        def finish(b):
+            n, bb = divmod(b, 2)
+            m1, m2 = state[("m", b)]
+            if bb == 0:
+                y = ypool.tile([P, 2, 4, P], F32, tag="y")
+                state[("y", n)] = y
+            y = state[("y", n)]
+            js = slice(2 * bb, 2 * bb + 2)
+            m1v = m1[:].rearrange("p (a q f) -> p a q f", a=2, q=2)
+            m2v = m2[:].rearrange("p (a q f) -> p a q f", a=2, q=2)
+            cs = slice(256 * bb, 256 * bb + 256)
+            if b == BATCHES - 1:
+                for q in range(2):
+                    nc.vector.tensor_tensor(out=y[:, q, js, :], in0=m1v[:, :, q, :], in1=m2v[:, :, q, :], op=ALU.add)
+                    nc.sync.dma_start(out=out_v[q][n][:, cs], in_=y[:, q, js, :].rearrange("p j f -> p (j f)"))
+                return
+            nc.gpsimd.tensor_tensor(out=y[:, :, js, :].rearrange("p q a f -> p a q f"), in0=m1v, in1=m2v, op=ALU.add)
+            if n == CHUNKS - 1:
+                for q in range(2):
+                    nc.sync.dma_start(out=out_v[q][n][:, cs], in_=y[:, q, js, :].rearrange("p j f -> p (j f)"))
+            elif bb == 1:
+                for q in range(2):
+                    nc.sync.dma_start(out=out_v[q][n], in_=y[:, q].rearrange("p j f -> p (j f)"))
+                if n + AHEAD < CHUNKS:
+                    load(n + AHEAD)
+
+        w_transpose(0)
+        w_transpose(1)
+        w_copy(0)
+        w_copy(1)
+        tables_scalar()
+        transposes(0)
+        w_quantise(0, 256)
+        w_transpose(2)
+        w_copy(2)
+        w_quantise(256, 384)
+        quantise(0)
+        transposes(1)
+        tables_vector()
+        quantise(1)
+        t_done = 1
+        q_done = 1
+        for k in range(-2, BATCHES, 2):
+            for b in (k, k + 1):
+                if b >= 0:
+                    products(b)
+            t_up = min(BATCHES - 1, k + 5) if k >= 0 else 3
+            while t_done < t_up:
+                t_done += 1
+                transposes(t_done)
+            for b in (k, k + 1):
+                if b >= 0:
+                    rotate(b)
+                    while q_done < min(BATCHES - 1, b + 3):
+                        q_done += 1
+                        quantise(q_done)
+                    finish(b)

@@ -47,6 +47,7 @@ def tile_attention_pa_t_kernel(tc, emb, W1, W2, W3, out_0, out_1, out_2):
         kpool = ctx.enter_context(tc.tile_pool(name="kpool", bufs=5))
         mpool = ctx.enter_context(tc.tile_pool(name="mpool", bufs=4))
         ypool = ctx.enter_context(tc.tile_pool(name="ypool", bufs=6))
+        ppool = ctx.enter_context(tc.tile_pool(name="ppool", bufs=4))
         ps_t = ctx.enter_context(tc.psum_pool(name="ps_t", bufs=4))
         ps_qk = ctx.enter_context(tc.psum_pool(name="ps_qk", bufs=2))
         ps_v = ctx.enter_context(tc.psum_pool(name="ps_v", bufs=2))
@@ -156,17 +157,24 @@ def tile_attention_pa_t_kernel(tc, emb, W1, W2, W3, out_0, out_1, out_2):
                     in_=w_grp[:, g, lo:hi, :].rearrange("p f t -> p (f t)"),
                 )
 
+        def permute(b):
+            n, bb = divmod(b, 2)
+            x32 = state[("x", n)][:].bitcast(F32)
+            xp = ppool.tile([P, 2, 2, P], F32, tag="xp")
+            nc.scalar.copy(out=xp[:], in_=x32[:, 2 * bb:2 * bb + 2, 256:512].rearrange("p j (r u) -> p j u r", u=2))
+            state[("xp", b)] = xp
+
         def transposes(b):
             n, bb = divmod(b, 2)
             x32 = state[("x", n)][:].bitcast(F32)
+            xp = state[("xp", b)]
             grp = gpool.tile([P, 2, 2, P, 4], BF16, tag="grp", align_bytes=64)
             grp32 = grp[:].bitcast(F32)
             for jj in range(2):
                 tp = ps_t.tile([P, 4, P], F32, tag="tp")
                 for wb in range(4):
-                    nc.tensor.transpose(
-                        out=tp[:, wb, :], in_=x32[:, 2 * bb + jj, 256 * (wb // 2) + wb % 2:256 * (wb // 2 + 1):2], identity=ident[:]
-                    )
+                    words = x32[:, 2 * bb + jj, wb:256:2] if wb < 2 else xp[:, jj, wb - 2, :]
+                    nc.tensor.transpose(out=tp[:, wb, :], in_=words, identity=ident[:])
                 nc.scalar.copy(out=grp32[:, jj], in_=tp[:].rearrange("p (g u) r -> p g r u", u=2))
             state[("grp", b)] = grp
 
@@ -255,13 +263,17 @@ def tile_attention_pa_t_kernel(tc, emb, W1, W2, W3, out_0, out_1, out_2):
         w_copy(0)
         w_copy(1)
         tables_scalar()
+        permute(0)
         transposes(0)
+        permute(1)
         w_quantise(0, 256)
         w_transpose(2)
         w_copy(2)
         w_quantise(256, 384)
         quantise(0)
         transposes(1)
+        permute(2)
+        permute(3)
         tables_vector()
         quantise(1)
         t_done = 1
@@ -274,6 +286,8 @@ def tile_attention_pa_t_kernel(tc, emb, W1, W2, W3, out_0, out_1, out_2):
             while t_done < t_up:
                 t_done += 1
                 transposes(t_done)
+                if t_done + 2 < BATCHES:
+                    permute(t_done + 2)
             for b in (k, k + 1):
                 if b >= 0:
                     rotate(b)

@@ -20,7 +20,7 @@ PI = 3.141592653589793
 NFREQ = 16
 CHUNKS = 16
 BATCHES = 32
-AHEAD = 10
+AHEAD = 12
 
 
 def round_bits(x, bits):
@@ -43,8 +43,8 @@ def tile_attention_pa_t_kernel(tc, emb, W1, W2, W3, out_0, out_1, out_2):
     with ExitStack() as ctx:
         const = ctx.enter_context(tc.tile_pool(name="const", bufs=1))
         xpool = ctx.enter_context(tc.tile_pool(name="xpool", bufs=AHEAD))
-        gpool = ctx.enter_context(tc.tile_pool(name="gpool", bufs=4))
-        kpool = ctx.enter_context(tc.tile_pool(name="kpool", bufs=5))
+        gpool = ctx.enter_context(tc.tile_pool(name="gpool", bufs=6))
+        kpool = ctx.enter_context(tc.tile_pool(name="kpool", bufs=6))
         mpool = ctx.enter_context(tc.tile_pool(name="mpool", bufs=4))
         ypool = ctx.enter_context(tc.tile_pool(name="ypool", bufs=6))
         ppool = ctx.enter_context(tc.tile_pool(name="ppool", bufs=4))
@@ -94,10 +94,15 @@ def tile_attention_pa_t_kernel(tc, emb, W1, W2, W3, out_0, out_1, out_2):
         tl = const.tile([P, 16, NFREQ], F32)
         for i in range(NFREQ):
             nc.vector.tensor_scalar_mul(out=th[:, :, i], in0=s_f[:], scalar1=PHI_HI[i])
-            nc.scalar.mul(out=tl[:, :, i], in_=s_f[:], mul=PHI_LO[i])
-        tq = const.tile([P, 256], F32)
+            if i < 6:
+                nc.gpsimd.tensor_scalar(
+                    out=tl[:, :, i], in0=s_f[:], scalar1=PHI_LO[i], scalar2=0.0, op0=ALU.mult, op1=ALU.add
+                )
+            else:
+                nc.scalar.mul(out=tl[:, :, i], in_=s_f[:], mul=PHI_LO[i])
         th2 = th[:].rearrange("p m i -> p (m i)")
         tl2 = tl[:].rearrange("p m i -> p (m i)")
+        tq = const.tile([P, 256], F32)
         nc.vector.scalar_tensor_tensor(out=tq[:], in0=th2, scalar=0.25, in1=tl2, op0=ALU.add, op1=ALU.add)
         n_i = const.tile([P, 256], I32)
         nc.vector.tensor_copy(out=n_i[:], in_=tq[:])
@@ -109,74 +114,84 @@ def tile_attention_pa_t_kernel(tc, emb, W1, W2, W3, out_0, out_1, out_2):
         qs = const.tile([P, 256], F32)
         hs2 = const.tile([P, 256], F32)
         qs2 = const.tile([P, 256], F32)
-
-        def tables_scalar():
-            nc.scalar.activation(out=hs[:], in_=fr2[:], func=ACT.Sin, scale=PI)
-            nc.scalar.activation(out=qs[:], in_=fr2[:], func=ACT.Sin, scale=PI / 2.0)
-            nc.scalar.square(out=hs2[:], in_=hs[:])
-            nc.scalar.square(out=qs2[:], in_=qs[:])
-
+        nc.scalar.activation(out=hs[:], in_=fr2[:], func=ACT.Sin, scale=PI)
+        nc.scalar.activation(out=qs[:], in_=fr2[:], func=ACT.Sin, scale=PI / 2.0)
+        nc.scalar.square(out=hs2[:], in_=hs[:])
+        nc.scalar.square(out=qs2[:], in_=qs[:])
         ctab = const.tile([P, 4, P], F32)
         stab = const.tile([P, 4, P], F32)
+        cpf = const.tile([P, 256], F32)
+        ctab_v = ctab[:].rearrange("p j (n two) -> p (j n) two", two=2)
+        stab_v = stab[:].rearrange("p j (n two) -> p (j n) two", two=2)
+        nc.gpsimd.tensor_scalar(out=cpf[:], in0=qs2[:], scalar1=-4.0, scalar2=2.0, op0=ALU.mult, op1=ALU.add)
+        nc.gpsimd.tensor_scalar(
+            out=ctab_v, in0=hs2[:].unsqueeze(2).to_broadcast([P, 256, 2]),
+            scalar1=-2.0, scalar2=1.0, op0=ALU.mult, op1=ALU.add,
+        )
+        nc.gpsimd.tensor_tensor(out=stab_v[:, :, 1], in0=hs[:], in1=cpf[:], op=ALU.mult)
+        nc.gpsimd.tensor_scalar(
+            out=stab_v[:, :, 0], in0=stab_v[:, :, 1], scalar1=-1.0, scalar2=0.0, op0=ALU.mult, op1=ALU.add
+        )
 
-        def tables_vector():
-            cpf = const.tile([P, 256], F32)
-            nc.vector.tensor_scalar(out=cpf[:], in0=qs2[:], scalar1=-4.0, scalar2=2.0, op0=ALU.mult, op1=ALU.add)
-            ctab_v = ctab[:].rearrange("p j (n two) -> p (j n) two", two=2)
-            stab_v = stab[:].rearrange("p j (n two) -> p (j n) two", two=2)
-            nc.vector.tensor_scalar(
-                out=ctab_v, in0=hs2[:].unsqueeze(2).to_broadcast([P, 256, 2]),
-                scalar1=-2.0, scalar2=1.0, op0=ALU.mult, op1=ALU.add,
-            )
-            nc.vector.tensor_tensor(out=stab_v[:, :, 1], in0=hs[:], in1=cpf[:], op=ALU.mult)
-            nc.vector.tensor_scalar_mul(out=stab_v[:, :, 0], in0=stab_v[:, :, 1], scalar1=-1.0)
-
-        w_grp = const.tile([P, 2, 384, 4], BF16, align_bytes=64)
-        w_grp32 = w_grp[:].bitcast(F32)
         w_raw32 = w_raw[:].bitcast(F32)
+        w_grp = [const.tile([P, 2, P, 4], BF16, align_bytes=64, name="w_grp%d" % w) for w in range(3)]
         w_codes = const.tile([P, 2, 384], U32, align_bytes=64)
         w_scales = const.tile([P, 2, 384], U8, align_bytes=64)
 
         def w_transpose(w):
             tp = ps_t.tile([P, 4, P], F32, tag="tp")
             for wb in range(4):
-                nc.tensor.transpose(out=tp[:, wb, :], in_=w_raw32[:, w, 256 * (wb // 2) + wb % 2:256 * (wb // 2 + 1):2], identity=ident[:])
+                g, u = divmod(wb, 2)
+                nc.tensor.transpose(
+                    out=tp[:, wb, :], in_=w_raw32[:, w, 256 * g + u:256 * g + 256:2], identity=ident[:]
+                )
             state[("wtp", w)] = tp
 
         def w_copy(w):
             nc.vector.tensor_copy(
-                out=w_grp32[:, :, w * P:(w + 1) * P, :],
+                out=w_grp[w][:].bitcast(F32),
                 in_=state[("wtp", w)][:].rearrange("p (g u) r -> p g r u", u=2),
             )
 
-        def w_quantise(lo, hi):
+        def w_quantise(w):
             for g in range(2):
                 nc.vector.quantize_mx(
-                    out=w_codes[:, g, lo:hi].bitcast(FP8X4),
-                    scales=w_scales[:, g, lo:hi],
-                    in_=w_grp[:, g, lo:hi, :].rearrange("p f t -> p (f t)"),
+                    out=w_codes[:, g, w * P:(w + 1) * P].bitcast(FP8X4),
+                    scales=w_scales[:, g, w * P:(w + 1) * P],
+                    in_=w_grp[w][:, g].rearrange("p f t -> p (f t)"),
                 )
 
+        def permuted(b):
+            return b > 2
+
         def permute(b):
+            if b >= BATCHES or not permuted(b):
+                return
             n, bb = divmod(b, 2)
             x32 = state[("x", n)][:].bitcast(F32)
             xp = ppool.tile([P, 2, 2, P], F32, tag="xp")
-            nc.scalar.copy(out=xp[:], in_=x32[:, 2 * bb:2 * bb + 2, 256:512].rearrange("p j (r u) -> p j u r", u=2))
+            nc.scalar.copy(
+                out=xp[:], in_=x32[:, 2 * bb:2 * bb + 2, 256:512].rearrange("p j (r u) -> p j u r", u=2)
+            )
             state[("xp", b)] = xp
 
         def transposes(b):
             n, bb = divmod(b, 2)
             x32 = state[("x", n)][:].bitcast(F32)
-            xp = state[("xp", b)]
             grp = gpool.tile([P, 2, 2, P, 4], BF16, tag="grp", align_bytes=64)
             grp32 = grp[:].bitcast(F32)
             for jj in range(2):
                 tp = ps_t.tile([P, 4, P], F32, tag="tp")
                 for wb in range(4):
-                    words = x32[:, 2 * bb + jj, wb:256:2] if wb < 2 else xp[:, jj, wb - 2, :]
+                    g, u = divmod(wb, 2)
+                    if g == 1 and permuted(b):
+                        words = state[("xp", b)][:, jj, u, :]
+                    else:
+                        words = x32[:, 2 * bb + jj, 256 * g + u:256 * g + 256:2]
                     nc.tensor.transpose(out=tp[:, wb, :], in_=words, identity=ident[:])
                 nc.scalar.copy(out=grp32[:, jj], in_=tp[:].rearrange("p (g u) r -> p g r u", u=2))
             state[("grp", b)] = grp
+            permute(b + 2)
 
         def quantise(b):
             grp = state[("grp", b)]
@@ -262,36 +277,30 @@ def tile_attention_pa_t_kernel(tc, emb, W1, W2, W3, out_0, out_1, out_2):
         w_transpose(1)
         w_copy(0)
         w_copy(1)
-        tables_scalar()
-        permute(0)
         transposes(0)
-        permute(1)
-        w_quantise(0, 256)
+        w_quantise(0)
+        w_quantise(1)
+        quantise(0)
         w_transpose(2)
         w_copy(2)
-        w_quantise(256, 384)
-        quantise(0)
+        w_quantise(2)
         transposes(1)
-        permute(2)
-        permute(3)
-        tables_vector()
         quantise(1)
-        t_done = 1
-        q_done = 1
-        for k in range(-2, BATCHES, 2):
-            for b in (k, k + 1):
-                if b >= 0:
-                    products(b)
-            t_up = min(BATCHES - 1, k + 5) if k >= 0 else 3
-            while t_done < t_up:
-                t_done += 1
-                transposes(t_done)
-                if t_done + 2 < BATCHES:
-                    permute(t_done + 2)
-            for b in (k, k + 1):
-                if b >= 0:
-                    rotate(b)
-                    while q_done < min(BATCHES - 1, b + 3):
-                        q_done += 1
-                        quantise(q_done)
-                    finish(b)
+        transposes(2)
+        products(0)
+        transposes(3)
+        transposes(4)
+        rotate(0)
+        quantise(2)
+        finish(0)
+        for k in range(1, BATCHES, 2):
+            pair = range(k, min(k + 2, BATCHES))
+            for b in pair:
+                products(b)
+            for b in range(k + 4, min(k + 6, BATCHES)):
+                transposes(b)
+            for b in pair:
+                rotate(b)
+                if b + 2 < BATCHES:
+                    quantise(b + 2)
+                finish(b)

@@ -21,6 +21,7 @@ NFREQ = 16
 CHUNKS = 16
 BATCHES = 32
 AHEAD = 12
+GCOLS = 96
 
 
 def round_bits(x, bits):
@@ -44,7 +45,7 @@ def tile_attention_pa_t_kernel(tc, emb, W1, W2, W3, out_0, out_1, out_2):
         const = ctx.enter_context(tc.tile_pool(name="const", bufs=1))
         xpool = ctx.enter_context(tc.tile_pool(name="xpool", bufs=AHEAD))
         gpool = ctx.enter_context(tc.tile_pool(name="gpool", bufs=6))
-        kpool = ctx.enter_context(tc.tile_pool(name="kpool", bufs=6))
+        kpool = ctx.enter_context(tc.tile_pool(name="kpool", bufs=7))
         mpool = ctx.enter_context(tc.tile_pool(name="mpool", bufs=4))
         ypool = ctx.enter_context(tc.tile_pool(name="ypool", bufs=6))
         ppool = ctx.enter_context(tc.tile_pool(name="ppool", bufs=4))
@@ -161,17 +162,18 @@ def tile_attention_pa_t_kernel(tc, emb, W1, W2, W3, out_0, out_1, out_2):
                     in_=w_grp[w][:, g].rearrange("p f t -> p (f t)"),
                 )
 
-        def permuted(b):
-            return b > 2
+        def first_permuted(b):
+            return 2 if b < 3 else 1 - b % 2
 
         def permute(b):
-            if b >= BATCHES or not permuted(b):
+            if b >= BATCHES or first_permuted(b) > 1:
                 return
+            j0 = first_permuted(b)
             n, bb = divmod(b, 2)
             x32 = state[("x", n)][:].bitcast(F32)
             xp = ppool.tile([P, 2, 2, P], F32, tag="xp")
             nc.scalar.copy(
-                out=xp[:], in_=x32[:, 2 * bb:2 * bb + 2, 256:512].rearrange("p j (r u) -> p j u r", u=2)
+                out=xp[:, j0:], in_=x32[:, 2 * bb + j0:2 * bb + 2, 256:512].rearrange("p j (r u) -> p j u r", u=2)
             )
             state[("xp", b)] = xp
 
@@ -184,7 +186,7 @@ def tile_attention_pa_t_kernel(tc, emb, W1, W2, W3, out_0, out_1, out_2):
                 tp = ps_t.tile([P, 4, P], F32, tag="tp")
                 for wb in range(4):
                     g, u = divmod(wb, 2)
-                    if g == 1 and permuted(b):
+                    if g == 1 and jj >= first_permuted(b):
                         words = state[("xp", b)][:, jj, u, :]
                     else:
                         words = x32[:, 2 * bb + jj, 256 * g + u:256 * g + 256:2]
@@ -247,23 +249,38 @@ def tile_attention_pa_t_kernel(tc, emb, W1, W2, W3, out_0, out_1, out_2):
             )
             state[("m", b)] = (m1, m2)
 
+        def halves(b):
+            return [t[:].rearrange("p (a q f) -> p a q f", a=2, q=2) for t in state[("m", b)]]
+
         def finish(b):
             n, bb = divmod(b, 2)
-            m1, m2 = state[("m", b)]
+            m1v, m2v = halves(b)
             if bb == 0:
                 y = ypool.tile([P, 2, 4, P], F32, tag="y")
                 state[("y", n)] = y
             y = state[("y", n)]
             js = slice(2 * bb, 2 * bb + 2)
-            m1v = m1[:].rearrange("p (a q f) -> p a q f", a=2, q=2)
-            m2v = m2[:].rearrange("p (a q f) -> p a q f", a=2, q=2)
             cs = slice(256 * bb, 256 * bb + 256)
             if b == BATCHES - 1:
                 for q in range(2):
                     nc.vector.tensor_tensor(out=y[:, q, js, :], in0=m1v[:, :, q, :], in1=m2v[:, :, q, :], op=ALU.add)
                     nc.sync.dma_start(out=out_v[q][n][:, cs], in_=y[:, q, js, :].rearrange("p j f -> p (j f)"))
                 return
-            nc.gpsimd.tensor_tensor(out=y[:, :, js, :].rearrange("p q a f -> p a q f"), in0=m1v, in1=m2v, op=ALU.add)
+            nc.gpsimd.tensor_tensor(
+                out=y[:, :, js, :GCOLS].rearrange("p q a f -> p a q f"),
+                in0=m1v[:, :, :, :GCOLS], in1=m2v[:, :, :, :GCOLS], op=ALU.add,
+            )
+
+        def finish_vector(b):
+            n, bb = divmod(b, 2)
+            m1v, m2v = halves(b)
+            y = state[("y", n)]
+            js = slice(2 * bb, 2 * bb + 2)
+            cs = slice(256 * bb, 256 * bb + 256)
+            nc.vector.tensor_tensor(
+                out=y[:, :, js, GCOLS:].rearrange("p q a f -> p a q f"),
+                in0=m1v[:, :, :, GCOLS:], in1=m2v[:, :, :, GCOLS:], op=ALU.add,
+            )
             if n == CHUNKS - 1:
                 for q in range(2):
                     nc.sync.dma_start(out=out_v[q][n][:, cs], in_=y[:, q, js, :].rearrange("p j f -> p (j f)"))
@@ -293,6 +310,7 @@ def tile_attention_pa_t_kernel(tc, emb, W1, W2, W3, out_0, out_1, out_2):
         rotate(0)
         quantise(2)
         finish(0)
+        q_done = 2
         for k in range(1, BATCHES, 2):
             pair = range(k, min(k + 2, BATCHES))
             for b in pair:
@@ -301,6 +319,8 @@ def tile_attention_pa_t_kernel(tc, emb, W1, W2, W3, out_0, out_1, out_2):
                 transposes(b)
             for b in pair:
                 rotate(b)
-                if b + 2 < BATCHES:
-                    quantise(b + 2)
+                finish_vector(b - 1)
+                while q_done < min(b + 3, BATCHES - 1):
+                    q_done += 1
+                    quantise(q_done)
                 finish(b)

@@ -21,7 +21,7 @@ NFREQ = 16
 CHUNKS = 16
 BATCHES = 32
 AHEAD = 12
-GCOLS = 96
+GCOLS = 80
 
 
 def round_bits(x, bits):
@@ -95,10 +95,9 @@ def tile_attention_pa_t_kernel(tc, emb, W1, W2, W3, out_0, out_1, out_2):
         tl = const.tile([P, 16, NFREQ], F32)
         for i in range(NFREQ):
             nc.vector.tensor_scalar_mul(out=th[:, :, i], in0=s_f[:], scalar1=PHI_HI[i])
-            if i < 6:
-                nc.gpsimd.tensor_scalar(
-                    out=tl[:, :, i], in0=s_f[:], scalar1=PHI_LO[i], scalar2=0.0, op0=ALU.mult, op1=ALU.add
-                )
+        for i in range(NFREQ):
+            if i < 8:
+                nc.vector.tensor_scalar_mul(out=tl[:, :, i], in0=s_f[:], scalar1=PHI_LO[i])
             else:
                 nc.scalar.mul(out=tl[:, :, i], in_=s_f[:], mul=PHI_LO[i])
         th2 = th[:].rearrange("p m i -> p (m i)")
@@ -121,18 +120,20 @@ def tile_attention_pa_t_kernel(tc, emb, W1, W2, W3, out_0, out_1, out_2):
         nc.scalar.square(out=qs2[:], in_=qs[:])
         ctab = const.tile([P, 4, P], F32)
         stab = const.tile([P, 4, P], F32)
-        cpf = const.tile([P, 256], F32)
         ctab_v = ctab[:].rearrange("p j (n two) -> p (j n) two", two=2)
         stab_v = stab[:].rearrange("p j (n two) -> p (j n) two", two=2)
-        nc.gpsimd.tensor_scalar(out=cpf[:], in0=qs2[:], scalar1=-4.0, scalar2=2.0, op0=ALU.mult, op1=ALU.add)
         nc.gpsimd.tensor_scalar(
             out=ctab_v, in0=hs2[:].unsqueeze(2).to_broadcast([P, 256, 2]),
             scalar1=-2.0, scalar2=1.0, op0=ALU.mult, op1=ALU.add,
         )
-        nc.gpsimd.tensor_tensor(out=stab_v[:, :, 1], in0=hs[:], in1=cpf[:], op=ALU.mult)
-        nc.gpsimd.tensor_scalar(
-            out=stab_v[:, :, 0], in0=stab_v[:, :, 1], scalar1=-1.0, scalar2=0.0, op0=ALU.mult, op1=ALU.add
-        )
+
+        def sine_table():
+            hc = const.tile([P, 256], F32)
+            nc.vector.scalar_tensor_tensor(
+                out=hc[:], in0=qs2[:], scalar=0.5, in1=hs[:], op0=ALU.subtract, op1=ALU.mult
+            )
+            nc.vector.tensor_scalar_mul(out=stab_v[:, :, 0], in0=hc[:], scalar1=4.0)
+            nc.vector.tensor_scalar_mul(out=stab_v[:, :, 1], in0=hc[:], scalar1=-4.0)
 
         w_raw32 = w_raw[:].bitcast(F32)
         w_grp = [const.tile([P, 2, P, 4], BF16, align_bytes=64, name="w_grp%d" % w) for w in range(3)]
@@ -163,7 +164,7 @@ def tile_attention_pa_t_kernel(tc, emb, W1, W2, W3, out_0, out_1, out_2):
                 )
 
         def first_permuted(b):
-            return 2 if b < 3 else 1 - b % 2
+            return 0 if b > 2 and b % 2 == 1 else 2
 
         def permute(b):
             if b >= BATCHES or first_permuted(b) > 1:
@@ -208,14 +209,20 @@ def tile_attention_pa_t_kernel(tc, emb, W1, W2, W3, out_0, out_1, out_2):
         def products(b):
             n, bb = divmod(b, 2)
             codes, scales = state[("q", b)]
-            qk = ps_qk.tile([P, 2, 256], F32, tag="qk")
-            vb = ps_v.tile([P, 2, P], F32, tag="vb")
-            for jj in range(2):
-                for g in range(2):
-                    c0 = (jj * 2 + g) * P
-                    for dst, lo, hi in ((qk[:, jj, :], 0, 256), (vb[:, jj, :], 256, 384)):
+            if b < BATCHES - 2:
+                qk = ps_qk.tile([P, 2, 256], F32, tag="qk")
+            else:
+                qk = ps_t.tile([P, 2, 256], F32, tag="tp")
+            if bb == 0:
+                vb = ps_v.tile([P, 4, P], F32, tag="vb")
+                state[("vb", n)] = vb
+            vb = state[("vb", n)]
+            for dst, lo, hi in ((qk[:], 0, 256), (vb[:, 2 * bb:2 * bb + 2, :], 256, 384)):
+                for jj in range(2):
+                    for g in range(2):
+                        c0 = (jj * 2 + g) * P
                         nc.tensor.matmul_mx(
-                            out=dst,
+                            out=dst[:, jj, :],
                             lhsT=codes[:, c0:c0 + P].bitcast(FP8X4),
                             lhsT_scale=scales[:, c0:c0 + P],
                             rhs=w_codes[:, g, lo:hi].bitcast(FP8X4),
@@ -223,12 +230,10 @@ def tile_attention_pa_t_kernel(tc, emb, W1, W2, W3, out_0, out_1, out_2):
                             start=(g == 0), stop=(g == 1),
                         )
             state[("qk", b)] = qk
-            if bb == 0:
-                yv = ypool.tile([P, 4, P], F32, tag="yv")
-                state[("yv", n)] = yv
-            nc.scalar.copy(out=state[("yv", n)][:, 2 * bb:2 * bb + 2, :], in_=vb[:])
             if bb == 1:
-                nc.sync.dma_start(out=out_v[2][n], in_=state[("yv", n)][:].rearrange("p j f -> p (j f)"))
+                yv = ypool.tile([P, 4, P], F32, tag="yv")
+                nc.scalar.copy(out=yv[:], in_=vb[:])
+                nc.sync.dma_start(out=out_v[2][n], in_=yv[:].rearrange("p j f -> p (j f)"))
 
         def rotate(b):
             n, bb = divmod(b, 2)
@@ -297,30 +302,28 @@ def tile_attention_pa_t_kernel(tc, emb, W1, W2, W3, out_0, out_1, out_2):
         transposes(0)
         w_quantise(0)
         w_quantise(1)
+        sine_table()
         quantise(0)
         w_transpose(2)
         w_copy(2)
         w_quantise(2)
         transposes(1)
         quantise(1)
-        transposes(2)
-        products(0)
-        transposes(3)
-        transposes(4)
-        rotate(0)
-        quantise(2)
-        finish(0)
-        q_done = 2
-        for k in range(1, BATCHES, 2):
-            pair = range(k, min(k + 2, BATCHES))
+        q_done = 1
+        t_done = 1
+        for k in range(-1, BATCHES, 2):
+            pair = range(max(k, 0), min(k + 2, BATCHES))
             for b in pair:
                 products(b)
-            for b in range(k + 4, min(k + 6, BATCHES)):
+            t_goal = min(k + 5, BATCHES - 1) if k > 0 else 3
+            for b in range(t_done + 1, t_goal + 1):
                 transposes(b)
+            t_done = t_goal
             for b in pair:
                 rotate(b)
-                finish_vector(b - 1)
-                while q_done < min(b + 3, BATCHES - 1):
+                if b > 0:
+                    finish_vector(b - 1)
+                while q_done < min(b + 3, t_done, BATCHES - 1):
                     q_done += 1
                     quantise(q_done)
                 finish(b)

@@ -21,7 +21,7 @@ NFREQ = 16
 CHUNKS = 16
 BATCHES = 32
 AHEAD = 12
-GCOLS = 80
+GCOLS = 96
 
 
 def round_bits(x, bits):
@@ -164,7 +164,7 @@ def tile_attention_pa_t_kernel(tc, emb, W1, W2, W3, out_0, out_1, out_2):
                 )
 
         def first_permuted(b):
-            return 0 if b > 2 and b % 2 == 1 else 2
+            return 2 if b < 3 else 1 - b % 2
 
         def permute(b):
             if b >= BATCHES or first_permuted(b) > 1:
@@ -309,21 +309,16 @@ def tile_attention_pa_t_kernel(tc, emb, W1, W2, W3, out_0, out_1, out_2):
         w_quantise(2)
         transposes(1)
         quantise(1)
+        transposes(2)
         q_done = 1
-        t_done = 1
-        for k in range(-1, BATCHES, 2):
-            pair = range(max(k, 0), min(k + 2, BATCHES))
-            for b in pair:
-                products(b)
-            t_goal = min(k + 5, BATCHES - 1) if k > 0 else 3
-            for b in range(t_done + 1, t_goal + 1):
-                transposes(b)
-            t_done = t_goal
-            for b in pair:
-                rotate(b)
-                if b > 0:
-                    finish_vector(b - 1)
-                while q_done < min(b + 3, t_done, BATCHES - 1):
-                    q_done += 1
-                    quantise(q_done)
-                finish(b)
+        for b in range(BATCHES):
+            products(b)
+            if b + 3 < BATCHES:
+                transposes(b + 3)
+            rotate(b)
+            if b > 0:
+                finish_vector(b - 1)
+            while q_done < min(b + 2, BATCHES - 1):
+                q_done += 1
+                quantise(q_done)
+            finish(b)

@@ -22,6 +22,7 @@ CHUNKS = 16
 BATCHES = 32
 AHEAD = 12
 GCOLS = 96
+WHOLE = 29
 
 
 def round_bits(x, bits):
@@ -64,14 +65,14 @@ def tile_attention_pa_t_kernel(tc, emb, W1, W2, W3, out_0, out_1, out_2):
         def load(n):
             x = xpool.tile([P, 4, E], BF16, tag="x")
             state[("x", n)] = x
-            if n > 0:
+            if n > 1:
                 nc.sync.dma_start(out=x[:].rearrange("p j k -> p (j k)"), in_=emb_v[n])
 
-        def load_half(bb):
-            x = state[("x", 0)]
+        def load_half(n, bb):
+            x = state[("x", n)]
             nc.sync.dma_start(
                 out=x[:, 2 * bb:2 * bb + 2, :].rearrange("p j k -> p (j k)"),
-                in_=emb_v[0][:, 2 * bb * E:(2 * bb + 2) * E],
+                in_=emb_v[n][:, 2 * bb * E:(2 * bb + 2) * E],
             )
 
         w_raw = const.tile([P, 3, E], BF16)
@@ -79,10 +80,13 @@ def tile_attention_pa_t_kernel(tc, emb, W1, W2, W3, out_0, out_1, out_2):
         load(0)
         nc.sync.dma_start(out=w_raw[:, 0, :], in_=w_aps[0])
         nc.sync.dma_start(out=w_raw[:, 1, :], in_=w_aps[1])
-        load_half(0)
+        load_half(0, 0)
         nc.sync.dma_start(out=w_raw[:, 2, :], in_=w_aps[2])
-        load_half(1)
-        for n in range(1, AHEAD):
+        load_half(0, 1)
+        load(1)
+        load_half(1, 0)
+        load_half(1, 1)
+        for n in range(2, AHEAD):
             load(n)
 
         zero = const.tile([P, 1], F32)
@@ -114,18 +118,23 @@ def tile_attention_pa_t_kernel(tc, emb, W1, W2, W3, out_0, out_1, out_2):
         qs = const.tile([P, 256], F32)
         hs2 = const.tile([P, 256], F32)
         qs2 = const.tile([P, 256], F32)
-        nc.scalar.activation(out=hs[:], in_=fr2[:], func=ACT.Sin, scale=PI)
-        nc.scalar.activation(out=qs[:], in_=fr2[:], func=ACT.Sin, scale=PI / 2.0)
-        nc.scalar.square(out=hs2[:], in_=hs[:])
-        nc.scalar.square(out=qs2[:], in_=qs[:])
+
+        def sines():
+            nc.scalar.activation(out=hs[:], in_=fr2[:], func=ACT.Sin, scale=PI)
+            nc.scalar.activation(out=qs[:], in_=fr2[:], func=ACT.Sin, scale=PI / 2.0)
+            nc.scalar.square(out=hs2[:], in_=hs[:])
+            nc.scalar.square(out=qs2[:], in_=qs[:])
+
         ctab = const.tile([P, 4, P], F32)
         stab = const.tile([P, 4, P], F32)
         ctab_v = ctab[:].rearrange("p j (n two) -> p (j n) two", two=2)
         stab_v = stab[:].rearrange("p j (n two) -> p (j n) two", two=2)
-        nc.gpsimd.tensor_scalar(
-            out=ctab_v, in0=hs2[:].unsqueeze(2).to_broadcast([P, 256, 2]),
-            scalar1=-2.0, scalar2=1.0, op0=ALU.mult, op1=ALU.add,
-        )
+
+        def cosine_table():
+            nc.gpsimd.tensor_scalar(
+                out=ctab_v, in0=hs2[:].unsqueeze(2).to_broadcast([P, 256, 2]),
+                scalar1=-2.0, scalar2=1.0, op0=ALU.mult, op1=ALU.add,
+            )
 
         def sine_table():
             hc = const.tile([P, 256], F32)
@@ -150,7 +159,8 @@ def tile_attention_pa_t_kernel(tc, emb, W1, W2, W3, out_0, out_1, out_2):
             state[("wtp", w)] = tp
 
         def w_copy(w):
-            nc.vector.tensor_copy(
+            copy = nc.scalar.copy if w < 2 else nc.vector.tensor_copy
+            copy(
                 out=w_grp[w][:].bitcast(F32),
                 in_=state[("wtp", w)][:].rearrange("p (g u) r -> p g r u", u=2),
             )
@@ -271,9 +281,10 @@ def tile_attention_pa_t_kernel(tc, emb, W1, W2, W3, out_0, out_1, out_2):
                     nc.vector.tensor_tensor(out=y[:, q, js, :], in0=m1v[:, :, q, :], in1=m2v[:, :, q, :], op=ALU.add)
                     nc.sync.dma_start(out=out_v[q][n][:, cs], in_=y[:, q, js, :].rearrange("p j f -> p (j f)"))
                 return
+            cols = GCOLS if b < WHOLE else P
             nc.gpsimd.tensor_tensor(
-                out=y[:, :, js, :GCOLS].rearrange("p q a f -> p a q f"),
-                in0=m1v[:, :, :, :GCOLS], in1=m2v[:, :, :, :GCOLS], op=ALU.add,
+                out=y[:, :, js, :cols].rearrange("p q a f -> p a q f"),
+                in0=m1v[:, :, :, :cols], in1=m2v[:, :, :, :cols], op=ALU.add,
             )
 
         def finish_vector(b):
@@ -282,10 +293,11 @@ def tile_attention_pa_t_kernel(tc, emb, W1, W2, W3, out_0, out_1, out_2):
             y = state[("y", n)]
             js = slice(2 * bb, 2 * bb + 2)
             cs = slice(256 * bb, 256 * bb + 256)
-            nc.vector.tensor_tensor(
-                out=y[:, :, js, GCOLS:].rearrange("p q a f -> p a q f"),
-                in0=m1v[:, :, :, GCOLS:], in1=m2v[:, :, :, GCOLS:], op=ALU.add,
-            )
+            if b < WHOLE:
+                nc.vector.tensor_tensor(
+                    out=y[:, :, js, GCOLS:].rearrange("p q a f -> p a q f"),
+                    in0=m1v[:, :, :, GCOLS:], in1=m2v[:, :, :, GCOLS:], op=ALU.add,
+                )
             if n == CHUNKS - 1:
                 for q in range(2):
                     nc.sync.dma_start(out=out_v[q][n][:, cs], in_=y[:, q, js, :].rearrange("p j f -> p (j f)"))
@@ -299,6 +311,8 @@ def tile_attention_pa_t_kernel(tc, emb, W1, W2, W3, out_0, out_1, out_2):
         w_transpose(1)
         w_copy(0)
         w_copy(1)
+        sines()
+        cosine_table()
         transposes(0)
         w_quantise(0)
         w_quantise(1)

from contextlib import ExitStack

import concourse.mybir as mybir
from concourse.masks import make_identity

F32 = mybir.dt.float32
BF16 = mybir.dt.bfloat16
I32 = mybir.dt.int32
U32 = mybir.dt.uint32
U8 = mybir.dt.uint8
FP8X4 = mybir.dt.float8_e4m3fn_x4
ALU = mybir.AluOpType
ACT = mybir.ActivationFunctionType

P = 128
E = 1024
TOKENS = 8192
FLOPS = 2 * TOKENS * E * 384
PI = 3.141592653589793
NFREQ = 16
CHUNKS = 16
BATCHES = 32
AHEAD = 12
GCOLS = 96
WHOLE = 29


def round_bits(x, bits):
    k = 1.0
    while x * k < 2.0 ** (bits - 1):
        k = k * 2.0
    return round(x * k) / k


PHI = [10000.0 ** (-i / 16.0) / (2.0 * PI) for i in range(NFREQ)]
PHI_HI = [round_bits(v, 12) for v in PHI]
PHI_LO = [PHI[i] - PHI_HI[i] for i in range(NFREQ)]


def tile_attention_pa_t_kernel(tc, emb, W1, W2, W3, out_0, out_1, out_2):
    nc = tc.nc
    emb_v = emb.rearrange("b (h p j) k -> (b h) p (j k)", h=4, p=P, j=4)
    out_v = [o.rearrange("b h (a x) d -> (b h) a (x d)", x=16) for o in (out_0, out_1, out_2)]

    with ExitStack() as ctx:
        const = ctx.enter_context(tc.tile_pool(name="const", bufs=1))
        xpool = ctx.enter_context(tc.tile_pool(name="xpool", bufs=AHEAD))
        gpool = ctx.enter_context(tc.tile_pool(name="gpool", bufs=6))
        kpool = ctx.enter_context(tc.tile_pool(name="kpool", bufs=7))
        mpool = ctx.enter_context(tc.tile_pool(name="mpool", bufs=4))
        ypool = ctx.enter_context(tc.tile_pool(name="ypool", bufs=6))
        ppool = ctx.enter_context(tc.tile_pool(name="ppool", bufs=4))
        ps_t = ctx.enter_context(tc.psum_pool(name="ps_t", bufs=4))
        ps_qk = ctx.enter_context(tc.psum_pool(name="ps_qk", bufs=2))
        ps_v = ctx.enter_context(tc.psum_pool(name="ps_v", bufs=2))

        s_i = const.tile([P, 16], I32)
        nc.gpsimd.iota(s_i[:], pattern=[[1, 16]], base=0, channel_multiplier=16)
        ident = const.tile([P, P], F32)
        make_identity(nc, ident[:])
        ctx.enter_context(tc.manual_schedule())

        state = {}

        def load(n):
            x = xpool.tile([P, 4, E], BF16, tag="x")
            state[("x", n)] = x
            if n > 1:
                nc.sync.dma_start(out=x[:].rearrange("p j k -> p (j k)"), in_=emb_v[n])

        def load_half(n, bb):
            x = state[("x", n)]
            nc.sync.dma_start(
                out=x[:, 2 * bb:2 * bb + 2, :].rearrange("p j k -> p (j k)"),
                in_=emb_v[n][:, 2 * bb * E:(2 * bb + 2) * E],
            )

        w_raw = const.tile([P, 3, E], BF16)
        w_aps = (W1, W2, W3)
        load(0)
        nc.sync.dma_start(out=w_raw[:, 0, :], in_=w_aps[0])
        nc.sync.dma_start(out=w_raw[:, 1, :], in_=w_aps[1])
        load_half(0, 0)
        nc.sync.dma_start(out=w_raw[:, 2, :], in_=w_aps[2])
        load_half(0, 1)
        load(1)
        load_half(1, 0)
        load_half(1, 1)
        for n in range(2, AHEAD):
            load(n)

        zero = const.tile([P, 1], F32)
        nc.vector.memset(zero[:], 0.0)
        warm = const.tile([P, 1], F32)
        nc.scalar.activation(out=warm[:], in_=zero[:], func=ACT.Sin, scale=1.0)
        s_f = const.tile([P, 16], F32)
        nc.vector.tensor_copy(out=s_f[:], in_=s_i[:])
        th = const.tile([P, 16, NFREQ], F32)
        tl = const.tile([P, 16, NFREQ], F32)
        for i in range(NFREQ):
            nc.vector.tensor_scalar_mul(out=th[:, :, i], in0=s_f[:], scalar1=PHI_HI[i])
        for i in range(NFREQ):
            if i < 8:
                nc.vector.tensor_scalar_mul(out=tl[:, :, i], in0=s_f[:], scalar1=PHI_LO[i])
            else:
                nc.scalar.mul(out=tl[:, :, i], in_=s_f[:], mul=PHI_LO[i])
        th2 = th[:].rearrange("p m i -> p (m i)")
        tl2 = tl[:].rearrange("p m i -> p (m i)")
        tq = const.tile([P, 256], F32)
        nc.vector.scalar_tensor_tensor(out=tq[:], in0=th2, scalar=0.25, in1=tl2, op0=ALU.add, op1=ALU.add)
        n_i = const.tile([P, 256], I32)
        nc.vector.tensor_copy(out=n_i[:], in_=tq[:])
        fr = const.tile([P, 256], F32)
        nc.vector.tensor_tensor(out=fr[:], in0=th2, in1=n_i[:], op=ALU.subtract)
        fr2 = const.tile([P, 256], F32)
        nc.vector.tensor_tensor(out=fr2[:], in0=fr[:], in1=tl2, op=ALU.add)
        hs = const.tile([P, 256], F32)
        qs = const.tile([P, 256], F32)
        hs2 = const.tile([P, 256], F32)
        qs2 = const.tile([P, 256], F32)

        def sines():
            nc.scalar.activation(out=hs[:], in_=fr2[:], func=ACT.Sin, scale=PI)
            nc.scalar.activation(out=qs[:], in_=fr2[:], func=ACT.Sin, scale=PI / 2.0)
            nc.scalar.square(out=hs2[:], in_=hs[:])
            nc.scalar.square(out=qs2[:], in_=qs[:])

        ctab = const.tile([P, 4, P], F32)
        stab = const.tile([P, 4, P], F32)
        ctab_v = ctab[:].rearrange("p j (n two) -> p (j n) two", two=2)
        stab_v = stab[:].rearrange("p j (n two) -> p (j n) two", two=2)

        def cosine_table():
            nc.gpsimd.tensor_scalar(
                out=ctab_v, in0=hs2[:].unsqueeze(2).to_broadcast([P, 256, 2]),
                scalar1=-2.0, scalar2=1.0, op0=ALU.mult, op1=ALU.add,
            )

        def sine_table():
            hc = const.tile([P, 256], F32)
            nc.vector.scalar_tensor_tensor(
                out=hc[:], in0=qs2[:], scalar=0.5, in1=hs[:], op0=ALU.subtract, op1=ALU.mult
            )
            nc.vector.tensor_scalar_mul(out=stab_v[:, :, 0], in0=hc[:], scalar1=4.0)
            nc.vector.tensor_scalar_mul(out=stab_v[:, :, 1], in0=hc[:], scalar1=-4.0)

        w_raw32 = w_raw[:].bitcast(F32)
        w_grp = [const.tile([P, 2, P, 4], BF16, align_bytes=64, name="w_grp%d" % w) for w in range(3)]
        w_codes = const.tile([P, 2, 384], U32, align_bytes=64)
        w_scales = const.tile([P, 2, 384], U8, align_bytes=64)

        def w_transpose(w):
            tp = ps_t.tile([P, 4, P], F32, tag="tp")
            for wb in range(4):
                g, u = divmod(wb, 2)
                nc.tensor.transpose(
                    out=tp[:, wb, :], in_=w_raw32[:, w, 256 * g + u:256 * g + 256:2], identity=ident[:]
                )
            state[("wtp", w)] = tp

        def w_copy(w):
            copy = nc.scalar.copy if w < 2 else nc.vector.tensor_copy
            copy(
                out=w_grp[w][:].bitcast(F32),
                in_=state[("wtp", w)][:].rearrange("p (g u) r -> p g r u", u=2),
            )

        def w_quantise(w):
            for g in range(2):
                nc.vector.quantize_mx(
                    out=w_codes[:, g, w * P:(w + 1) * P].bitcast(FP8X4),
                    scales=w_scales[:, g, w * P:(w + 1) * P],
                    in_=w_grp[w][:, g].rearrange("p f t -> p (f t)"),
                )

        def first_permuted(b):
            return 2 if b < 3 else 1 - b % 2

        def permute(b):
            if b >= BATCHES or first_permuted(b) > 1:
                return
            j0 = first_permuted(b)
            n, bb = divmod(b, 2)
            x32 = state[("x", n)][:].bitcast(F32)
            xp = ppool.tile([P, 2, 2, P], F32, tag="xp")
            nc.scalar.copy(
                out=xp[:, j0:], in_=x32[:, 2 * bb + j0:2 * bb + 2, 256:512].rearrange("p j (r u) -> p j u r", u=2)
            )
            state[("xp", b)] = xp

        def transposes(b):
            n, bb = divmod(b, 2)
            x32 = state[("x", n)][:].bitcast(F32)
            grp = gpool.tile([P, 2, 2, P, 4], BF16, tag="grp", align_bytes=64)
            grp32 = grp[:].bitcast(F32)
            for jj in range(2):
                tp = ps_t.tile([P, 4, P], F32, tag="tp")
                for wb in range(4):
                    g, u = divmod(wb, 2)
                    if g == 1 and jj >= first_permuted(b):
                        words = state[("xp", b)][:, jj, u, :]
                    else:
                        words = x32[:, 2 * bb + jj, 256 * g + u:256 * g + 256:2]
                    nc.tensor.transpose(out=tp[:, wb, :], in_=words, identity=ident[:])
                nc.scalar.copy(out=grp32[:, jj], in_=tp[:].rearrange("p (g u) r -> p g r u", u=2))
            state[("grp", b)] = grp
            permute(b + 2)

        def quantise(b):
            grp = state[("grp", b)]
            codes = kpool.tile([P, 512], U32, tag="codes", align_bytes=64)
            scales = kpool.tile([P, 512], U8, tag="scales", align_bytes=64)
            nc.vector.quantize_mx(
                out=codes[:].bitcast(FP8X4), scales=scales[:],
                in_=grp[:].rearrange("p a g r t -> p (a g r t)"),
            )
            state[("q", b)] = (codes, scales)

        def products(b):
            n, bb = divmod(b, 2)
            codes, scales = state[("q", b)]
            if b < BATCHES - 2:
                qk = ps_qk.tile([P, 2, 256], F32, tag="qk")
            else:
                qk = ps_t.tile([P, 2, 256], F32, tag="tp")
            if bb == 0:
                vb = ps_v.tile([P, 4, P], F32, tag="vb")
                state[("vb", n)] = vb
            vb = state[("vb", n)]
            for dst, lo, hi in ((qk[:], 0, 256), (vb[:, 2 * bb:2 * bb + 2, :], 256, 384)):
                for jj in range(2):
                    for g in range(2):
                        c0 = (jj * 2 + g) * P
                        nc.tensor.matmul_mx(
                            out=dst[:, jj, :],
                            lhsT=codes[:, c0:c0 + P].bitcast(FP8X4),
                            lhsT_scale=scales[:, c0:c0 + P],
                            rhs=w_codes[:, g, lo:hi].bitcast(FP8X4),
                            rhs_scale=w_scales[:, g, lo:hi],
                            start=(g == 0), stop=(g == 1),
                        )
            state[("qk", b)] = qk
            if bb == 1:
                yv = ypool.tile([P, 4, P], F32, tag="yv")
                nc.scalar.copy(out=yv[:], in_=vb[:])
                nc.sync.dma_start(out=out_v[2][n], in_=yv[:].rearrange("p j f -> p (j f)"))

        def rotate(b):
            n, bb = divmod(b, 2)
            qk = state[("qk", b)]
            shape5 = [P, 2, 2, 64, 2]
            m1 = mpool.tile([P, 512], F32, tag="m1")
            m2 = mpool.tile([P, 512], F32, tag="m2")
            js = slice(2 * bb, 2 * bb + 2)
            ct = ctab[:, js, :].rearrange("p a (n two) -> p a n two", two=2).unsqueeze(2).to_broadcast(shape5)
            st = stab[:, js, :].rearrange("p a (n two) -> p a n two", two=2).unsqueeze(2).to_broadcast(shape5)
            x5 = qk[:].rearrange("p a (q n two) -> p a q n two", q=2, two=2)
            nc.vector.tensor_tensor(
                out=m1[:].rearrange("p (a q n two) -> p a q n two", a=2, q=2, two=2), in0=x5, in1=ct, op=ALU.mult
            )
            nc.vector.tensor_tensor(
                out=m2[:].rearrange("p (a q n two) -> p a q n two", a=2, q=2, two=2),
                in0=x5[:, :, :, :, ::-1], in1=st, op=ALU.mult,
            )
            state[("m", b)] = (m1, m2)

        def halves(b):
            return [t[:].rearrange("p (a q f) -> p a q f", a=2, q=2) for t in state[("m", b)]]

        def finish(b):
            n, bb = divmod(b, 2)
            m1v, m2v = halves(b)
            if bb == 0:
                y = ypool.tile([P, 2, 4, P], F32, tag="y")
                state[("y", n)] = y
            y = state[("y", n)]
            js = slice(2 * bb, 2 * bb + 2)
            cs = slice(256 * bb, 256 * bb + 256)
            if b == BATCHES - 1:
                for q in range(2):
                    nc.vector.tensor_tensor(out=y[:, q, js, :], in0=m1v[:, :, q, :], in1=m2v[:, :, q, :], op=ALU.add)
                    nc.sync.dma_start(out=out_v[q][n][:, cs], in_=y[:, q, js, :].rearrange("p j f -> p (j f)"))
                return
            cols = GCOLS if b < WHOLE else P
            nc.gpsimd.tensor_tensor(
                out=y[:, :, js, :cols].rearrange("p q a f -> p a q f"),
                in0=m1v[:, :, :, :cols], in1=m2v[:, :, :, :cols], op=ALU.add,
            )

        def finish_vector(b):
            n, bb = divmod(b, 2)
            m1v, m2v = halves(b)
            y = state[("y", n)]
            js = slice(2 * bb, 2 * bb + 2)
            cs = slice(256 * bb, 256 * bb + 256)
            if b < WHOLE:
                nc.vector.tensor_tensor(
                    out=y[:, :, js, GCOLS:].rearrange("p q a f -> p a q f"),
                    in0=m1v[:, :, :, GCOLS:], in1=m2v[:, :, :, GCOLS:], op=ALU.add,
                )
            if n == CHUNKS - 1:
                for q in range(2):
                    nc.sync.dma_start(out=out_v[q][n][:, cs], in_=y[:, q, js, :].rearrange("p j f -> p (j f)"))
            elif bb == 1:
                for q in range(2):
                    nc.sync.dma_start(out=out_v[q][n], in_=y[:, q].rearrange("p j f -> p (j f)"))
                if n + AHEAD < CHUNKS:
                    load(n + AHEAD)

        w_transpose(0)
        w_transpose(1)
        w_copy(0)
        w_copy(1)
        sines()
        cosine_table()
        transposes(0)
        w_quantise(0)
        w_quantise(1)
        sine_table()
        quantise(0)
        w_transpose(2)
        w_copy(2)
        w_quantise(2)
        transposes(1)
        quantise(1)
        transposes(2)
        q_done = 1
        for b in range(BATCHES):
            products(b)
            if b + 3 < BATCHES:
                transposes(b + 3)
            rotate(b)
            if b > 0:
                finish_vector(b - 1)
            while q_done < min(b + 2, BATCHES - 1):
                q_done += 1
                quantise(q_done)
            finish(b)
